import numpy as np
import ml_dtypes


def mxq(x, axis, fmt="e4m3"):
    dtype, down = {"e4m3": (ml_dtypes.float8_e4m3fn, 7), "e5m2": (ml_dtypes.float8_e5m2, 14)}[fmt]
    v = np.moveaxis(np.asarray(x, np.float32).astype(ml_dtypes.bfloat16).astype(np.float64), axis, -1)
    blocks = v.reshape(v.shape[:-1] + (-1, 32))
    amax = np.abs(blocks).max(-1, keepdims=True)
    byte = np.maximum(np.where(amax > 0, np.frexp(amax)[1] - 1 + 127, 0) - down, 1)
    scale = np.exp2(byte - 127.0)
    codes = (blocks / scale).astype(np.float32).astype(dtype).astype(np.float64)
    return np.moveaxis((codes * scale).reshape(v.shape), -1, axis)


WIDE = False


def mx_kscale(k):
    if not WIDE:
        return np.ones(k)
    levels = np.array([10, -10, 5, -5, 0])
    a = np.random.permutation(np.resize(levels, k // 512 * 4)).reshape(k // 512, 4)
    idx = np.arange(k)
    return np.exp2(a[idx // 512, idx % 128 // 32])


BF16 = ml_dtypes.bfloat16


def bf(x):
    return np.asarray(x, np.float32).astype(BF16)


def f64(x):
    return np.asarray(x).astype(np.float64)


B, T, C, NH, NKV, HD, P = 1, 512, 2048, 16, 4, 128, 512


def rope(u, angles):
    up = u.reshape(u.shape[:-1] + (HD // 2, 2))
    cos = np.cos(angles)[None, :, None, :]
    sin = np.sin(angles)[None, :, None, :]
    u0, u1 = up[..., 0], up[..., 1]
    return np.stack([cos * u0 - sin * u1, sin * u0 + cos * u1], axis=-1).reshape(u.shape)


def setup_inputs():
    s = mx_kscale(C)
    return {"x": bf(np.random.standard_normal((B, T, C)) * s),
            "angles": bf(np.random.uniform(-np.pi, np.pi, (T, HD // 2))),
            "wq": bf(np.random.standard_normal((C, NH * HD)) * 0.5 / np.sqrt(C) / s[:, None]),
            "wk": bf(np.random.standard_normal((C, NKV * HD)) * 0.5 / np.sqrt(C) / s[:, None]),
            "wv": bf(np.random.standard_normal((C, NKV * HD)) / np.sqrt(C) / s[:, None])}


def reference(x, angles, wq, wk, wv):
    xq = mxq(f64(x), 2, "e4m3")
    a = f64(angles)
    q = (xq @ mxq(f64(wq), 0, "e4m3")).reshape(B, T, NH, HD)
    k = (xq @ mxq(f64(wk), 0, "e4m3")).reshape(B, T, NKV, HD)
    v = (xq @ mxq(f64(wv), 0, "e4m3")).reshape(B, T, NKV, HD)
    q = rope(q, a)
    k = rope(k, a)
    return q.transpose(0, 2, 1, 3), k.transpose(0, 2, 1, 3), v.transpose(0, 2, 1, 3)

@@ -1,0 +1,195 @@
+from contextlib import ExitStack
+
+import concourse.mybir as mybir
+from concourse.masks import make_identity
+
+F32 = mybir.dt.float32
+BF16 = mybir.dt.bfloat16
+U32 = mybir.dt.uint32
+U8 = mybir.dt.uint8
+FP8X4 = mybir.dt.float8_e4m3fn_x4
+ACT = mybir.ActivationFunctionType
+ALU = mybir.AluOpType
+
+P = 128
+PACK = 4
+K_PASS = P * PACK
+TOKENS = 512
+K = 2048
+HEAD = 128
+HALF = HEAD // 2
+Q_COLUMNS = 2048
+KV_COLUMNS = 512
+PASSES = K // K_PASS
+TOKEN_TILES = TOKENS // P
+BLOCK = 512
+HEADS = BLOCK // HEAD
+RUN = 4
+
+FLOPS = 2 * TOKENS * K * (Q_COLUMNS + 2 * KV_COLUMNS)
+
+assert TOKEN_TILES == PASSES
+
+
+def tile_groupqueryatention_pa_kernel(tc, x, angles, wq, wk, wv, out_0, out_1, out_2):
+    nc = tc.nc
+
+    blocks = [(wk, 0, out_1, 0, True)]
+    blocks += [(wq, g * BLOCK, out_0, g * HEADS, True) for g in range(Q_COLUMNS // BLOCK)]
+    blocks += [(wv, 0, out_2, 0, False)]
+    n_blocks = len(blocks)
+
+    with ExitStack() as stack:
+        consts = stack.enter_context(tc.tile_pool(name="consts", bufs=1))
+        raw_pool = stack.enter_context(tc.tile_pool(name="raw", bufs=n_blocks * PASSES))
+        x_grouped_pool = stack.enter_context(tc.tile_pool(name="x_grouped", bufs=2))
+        w_grouped_pool = stack.enter_context(tc.tile_pool(name="w_grouped", bufs=4))
+        w_mx_pool = stack.enter_context(tc.tile_pool(name="w_mx", bufs=2))
+        result_pool = stack.enter_context(tc.tile_pool(name="result", bufs=3))
+        odd_pool = stack.enter_context(tc.tile_pool(name="odd", bufs=2))
+        psum = stack.enter_context(tc.psum_pool(name="psum", bufs=8))
+        stack.enter_context(tc.manual_schedule())
+
+        angle = consts.tile([P, TOKEN_TILES, HALF], BF16)
+        nc.sync.dma_start(out=angle[:], in_=angles.rearrange("(p m) i -> p m i", m=TOKEN_TILES))
+
+        raw = {}
+
+        def load_block(b):
+            weight, column = blocks[b][0], blocks[b][1]
+            for c in range(PASSES):
+                rows = weight[c * K_PASS : (c + 1) * K_PASS, column : column + BLOCK]
+                raw[b, c] = raw_pool.tile([P, PACK, BLOCK], BF16, tag="raw", name="raw")
+                nc.sync.dma_start(
+                    out=raw[b, c][:], in_=rows.rearrange("(p j) n -> p j n", j=PACK)
+                )
+
+        load_block(0)
+        x_tokens = x[0].rearrange("(p m) k -> p m k", m=TOKEN_TILES)
+        x_sb = []
+        for m in range(TOKEN_TILES):
+            x_sb.append(consts.tile([P, K], BF16, name="x_sb%d" % m))
+            nc.sync.dma_start(out=x_sb[m][:], in_=x_tokens[:, m, :])
+        for b in range(1, n_blocks):
+            load_block(b)
+
+        identity = consts.tile([P, P], F32)
+        make_identity(nc, identity[:])
+
+        trig = consts.tile([P, 3, TOKEN_TILES, HALF], F32)
+        sin_half = consts.tile([P, TOKEN_TILES, HALF], F32)
+        sin_half_squared = consts.tile([P, TOKEN_TILES, HALF], F32)
+        nc.scalar.activation(out=trig[:, 0], in_=angle[:], func=ACT.Sin, scale=-1.0)
+        nc.scalar.activation(out=trig[:, 2], in_=angle[:], func=ACT.Sin)
+        nc.scalar.activation(out=sin_half[:], in_=angle[:], func=ACT.Sin, scale=0.5)
+        nc.gpsimd.tensor_tensor(
+            out=sin_half_squared[:], in0=sin_half[:], in1=sin_half[:], op=ALU.mult
+        )
+        nc.gpsimd.tensor_scalar(
+            out=trig[:, 1],
+            in0=sin_half_squared[:],
+            scalar1=-2.0,
+            scalar2=1.0,
+            op0=ALU.mult,
+            op1=ALU.add,
+        )
+
+        w_codes = {}
+        w_scales = {}
+
+        def prepare_chunk(b, c):
+            if c == 0:
+                w_codes[b] = w_mx_pool.tile(
+                    [P, PASSES, BLOCK], U32, tag="w_codes", name="w_codes", align_bytes=64
+                )
+                w_scales[b] = w_mx_pool.tile(
+                    [P, PASSES, BLOCK], U8, tag="w_scales", name="w_scales", align_bytes=64
+                )
+            copy = nc.vector.tensor_copy if (b == 0 and c % 2 == 0) else nc.scalar.copy
+            grouped = w_grouped_pool.tile([P, BLOCK, PACK], BF16, align_bytes=64)
+            copy(
+                out=grouped[:].rearrange("p (g i) j -> p g j i", i=RUN),
+                in_=raw[b, c][:].rearrange("p j (g i) -> p g j i", i=RUN),
+            )
+            nc.vector.quantize_mx(
+                out=w_codes[b][:, c, :].bitcast(FP8X4),
+                scales=w_scales[b][:, c, :],
+                in_=grouped[:].rearrange("p n j -> p (n j)"),
+            )
+
+        for c in range(PASSES):
+            prepare_chunk(0, c)
+
+        x_codes = []
+        x_scales = []
+        for m in range(TOKEN_TILES):
+            x_words = x_sb[m][:].bitcast(F32).rearrange("p (c q u) -> p c u q", c=PASSES, u=2)
+            grouped = x_grouped_pool.tile([P, PASSES * P * PACK], BF16, align_bytes=64)
+            grouped_words = grouped[:].bitcast(F32).rearrange("p (c t u) -> p c t u", c=PASSES, u=2)
+            for first in range(0, PASSES, 2):
+                bank = psum.tile([P, 2, 2, P], F32, tag="bank")
+                for c in range(2):
+                    for u in range(2):
+                        nc.tensor.transpose(bank[:, c, u, :], x_words[:, first + c, u, :], identity[:])
+                nc.scalar.copy(
+                    out=grouped_words[:, first : first + 2],
+                    in_=bank[:].rearrange("p c u t -> p c t u"),
+                )
+            x_codes.append(consts.tile([P, PASSES, P], U32, name="x_codes%d" % m, align_bytes=64))
+            x_scales.append(consts.tile([P, PASSES, P], U8, name="x_scales%d" % m, align_bytes=64))
+            nc.vector.quantize_mx(
+                out=x_codes[m][:].rearrange("p c t -> p (c t)").bitcast(FP8X4),
+                scales=x_scales[m][:].rearrange("p c t -> p (c t)"),
+                in_=grouped[:],
+            )
+
+        def multiply(b):
+            banks = []
+            for m in range(TOKEN_TILES):
+                acc = psum.tile([P, BLOCK], F32, tag="bank")
+                for c in range(PASSES):
+                    nc.tensor.matmul_mx(
+                        out=acc[:],
+                        lhsT=x_codes[m][:, c, :].bitcast(FP8X4),
+                        lhsT_scale=x_scales[m][:, c, :],
+                        rhs=w_codes[b][:, c, :].bitcast(FP8X4),
+                        rhs_scale=w_scales[b][:, c, :],
+                        start=(c == 0),
+                        stop=(c == PASSES - 1),
+                    )
+                banks.append(acc)
+            return banks
+
+        pair_shape = [P, HEADS, HALF, 2]
+        banks = multiply(0)
+        for b in range(n_blocks):
+            output, head, rotated = blocks[b][2], blocks[b][3], blocks[b][4]
+            result = result_pool.tile([P, HEADS, TOKEN_TILES, HEAD], F32)
+            if rotated:
+                odd_part = odd_pool.tile([P, HEADS, TOKEN_TILES, HEAD], F32)
+            for m in range(TOKEN_TILES):
+                if rotated:
+                    pairs = banks[m][:].rearrange("p (h i two) -> p h i two", h=HEADS, two=2)
+                    for part, which in ((result, 0), (odd_part, 1)):
+                        factors = trig[:, 1 - which : 3 - which, m, :].rearrange("p two i -> p i two")
+                        nc.vector.tensor_tensor(
+                            out=part[:, :, m, :].rearrange("p h (i two) -> p h i two", two=2),
+                            in0=pairs[:, :, :, which : which + 1].to_broadcast(pair_shape),
+                            in1=factors.unsqueeze(1).to_broadcast(pair_shape),
+                            op=ALU.mult,
+                        )
+                else:
+                    nc.scalar.copy(
+                        out=result[:, :, m, :],
+                        in_=banks[m][:].rearrange("p (h f) -> p h f", h=HEADS),
+                    )
+                if b + 1 < n_blocks:
+                    prepare_chunk(b + 1, m)
+            if rotated:
+                nc.vector.tensor_add(out=result[:], in0=result[:], in1=odd_part[:])
+            nc.sync.dma_start(
+                out=output[0, head : head + HEADS].rearrange("h (p m) f -> p h (m f)", m=TOKEN_TILES),
+                in_=result[:].rearrange("p h m f -> p h (m f)"),
+            )
+            if b + 1 < n_blocks:
+                banks = multiply(b + 1)

@@ -25,29 +25,29 @@ TOKEN_TILES = TOKENS // P
 BLOCK = 512
 HEADS = BLOCK // HEAD
 RUN = 4
+AHEAD = 2
+GPSIMD_BANKS = 2
+VECTOR_LAST_CHUNKS = 2
 
 FLOPS = 2 * TOKENS * K * (Q_COLUMNS + 2 * KV_COLUMNS)
-
-assert TOKEN_TILES == PASSES
 
 
 def tile_groupqueryatention_pa_kernel(tc, x, angles, wq, wk, wv, out_0, out_1, out_2):
     nc = tc.nc
 
-    blocks = [(wk, 0, out_1, 0, True)]
-    blocks += [(wq, g * BLOCK, out_0, g * HEADS, True) for g in range(Q_COLUMNS // BLOCK)]
-    blocks += [(wv, 0, out_2, 0, False)]
+    q_blocks = [(wq, g * BLOCK, out_0, g * HEADS, True) for g in range(Q_COLUMNS // BLOCK)]
+    blocks = [(wk, 0, out_1, 0, True)] + q_blocks[:-1] + [(wv, 0, out_2, 0, False)] + q_blocks[-1:]
     n_blocks = len(blocks)
 
     with ExitStack() as stack:
         consts = stack.enter_context(tc.tile_pool(name="consts", bufs=1))
         raw_pool = stack.enter_context(tc.tile_pool(name="raw", bufs=n_blocks * PASSES))
         x_grouped_pool = stack.enter_context(tc.tile_pool(name="x_grouped", bufs=2))
-        w_grouped_pool = stack.enter_context(tc.tile_pool(name="w_grouped", bufs=4))
-        w_mx_pool = stack.enter_context(tc.tile_pool(name="w_mx", bufs=2))
+        w_grouped_pool = stack.enter_context(tc.tile_pool(name="w_grouped", bufs=2 * PASSES))
+        w_mx_pool = stack.enter_context(tc.tile_pool(name="w_mx", bufs=AHEAD))
         result_pool = stack.enter_context(tc.tile_pool(name="result", bufs=3))
         odd_pool = stack.enter_context(tc.tile_pool(name="odd", bufs=2))
-        psum = stack.enter_context(tc.psum_pool(name="psum", bufs=8))
+        psum = stack.enter_context(tc.psum_pool(name="psum", bufs=AHEAD * TOKEN_TILES))
         stack.enter_context(tc.manual_schedule())
 
         angle = consts.tile([P, TOKEN_TILES, HALF], BF16)
@@ -55,23 +55,23 @@ def tile_groupqueryatention_pa_kernel(tc, x, angles, wq, wk, wv, out_0, out_1, o
 
         raw = {}
 
-        def load_block(b):
+        def load_chunk(b, c):
             weight, column = blocks[b][0], blocks[b][1]
-            for c in range(PASSES):
-                rows = weight[c * K_PASS : (c + 1) * K_PASS, column : column + BLOCK]
-                raw[b, c] = raw_pool.tile([P, PACK, BLOCK], BF16, tag="raw", name="raw")
-                nc.sync.dma_start(
-                    out=raw[b, c][:], in_=rows.rearrange("(p j) n -> p j n", j=PACK)
-                )
+            rows = weight[c * K_PASS : (c + 1) * K_PASS, column : column + BLOCK]
+            raw[b, c] = raw_pool.tile([P, PACK, BLOCK], BF16, tag="raw", name="raw")
+            nc.sync.dma_start(out=raw[b, c][:], in_=rows.rearrange("(p j) n -> p j n", j=PACK))
 
-        load_block(0)
+        for c in range(PASSES):
+            for b in range(AHEAD):
+                load_chunk(b, c)
         x_tokens = x[0].rearrange("(p m) k -> p m k", m=TOKEN_TILES)
         x_sb = []
         for m in range(TOKEN_TILES):
             x_sb.append(consts.tile([P, K], BF16, name="x_sb%d" % m))
             nc.sync.dma_start(out=x_sb[m][:], in_=x_tokens[:, m, :])
-        for b in range(1, n_blocks):
-            load_block(b)
+        for b in range(AHEAD, n_blocks):
+            for c in range(PASSES):
+                load_chunk(b, c)
 
         identity = consts.tile([P, P], F32)
         make_identity(nc, identity[:])
@@ -94,10 +94,22 @@ def tile_groupqueryatention_pa_kernel(tc, x, angles, wq, wk, wv, out_0, out_1, o
             op1=ALU.add,
         )
 
+        w_grouped = {}
         w_codes = {}
         w_scales = {}
 
-        def prepare_chunk(b, c):
+        def regroup(b, c):
+            on_vector = b == 0 or (c == PASSES - 1 and b <= VECTOR_LAST_CHUNKS)
+            copy = nc.vector.tensor_copy if on_vector else nc.scalar.copy
+            w_grouped[b, c] = w_grouped_pool.tile(
+                [P, BLOCK, PACK], BF16, tag="w_grouped", name="w_grouped", align_bytes=64
+            )
+            copy(
+                out=w_grouped[b, c][:].rearrange("p (g i) j -> p g j i", i=RUN),
+                in_=raw[b, c][:].rearrange("p j (g i) -> p g j i", i=RUN),
+            )
+
+        def quantise(b, c):
             if c == 0:
                 w_codes[b] = w_mx_pool.tile(
                     [P, PASSES, BLOCK], U32, tag="w_codes", name="w_codes", align_bytes=64
@@ -105,27 +117,27 @@ def tile_groupqueryatention_pa_kernel(tc, x, angles, wq, wk, wv, out_0, out_1, o
                 w_scales[b] = w_mx_pool.tile(
                     [P, PASSES, BLOCK], U8, tag="w_scales", name="w_scales", align_bytes=64
                 )
-            copy = nc.vector.tensor_copy if (b == 0 and c % 2 == 0) else nc.scalar.copy
-            grouped = w_grouped_pool.tile([P, BLOCK, PACK], BF16, align_bytes=64)
-            copy(
-                out=grouped[:].rearrange("p (g i) j -> p g j i", i=RUN),
-                in_=raw[b, c][:].rearrange("p j (g i) -> p g j i", i=RUN),
-            )
             nc.vector.quantize_mx(
                 out=w_codes[b][:, c, :].bitcast(FP8X4),
                 scales=w_scales[b][:, c, :],
-                in_=grouped[:].rearrange("p n j -> p (n j)"),
+                in_=w_grouped[b, c][:].rearrange("p n j -> p (n j)"),
             )
 
         for c in range(PASSES):
-            prepare_chunk(0, c)
+            for b in range(AHEAD):
+                regroup(b, c)
+            quantise(0, c)
+        for c in range(PASSES):
+            quantise(1, c)
 
         x_codes = []
         x_scales = []
         for m in range(TOKEN_TILES):
             x_words = x_sb[m][:].bitcast(F32).rearrange("p (c q u) -> p c u q", c=PASSES, u=2)
-            grouped = x_grouped_pool.tile([P, PASSES * P * PACK], BF16, align_bytes=64)
-            grouped_words = grouped[:].bitcast(F32).rearrange("p (c t u) -> p c t u", c=PASSES, u=2)
+            x_grouped = x_grouped_pool.tile([P, PASSES * P * PACK], BF16, align_bytes=64)
+            grouped_words = x_grouped[:].bitcast(F32).rearrange(
+                "p (c t u) -> p c t u", c=PASSES, u=2
+            )
             for first in range(0, PASSES, 2):
                 bank = psum.tile([P, 2, 2, P], F32, tag="bank")
                 for c in range(2):
@@ -140,7 +152,7 @@ def tile_groupqueryatention_pa_kernel(tc, x, angles, wq, wk, wv, out_0, out_1, o
             nc.vector.quantize_mx(
                 out=x_codes[m][:].rearrange("p c t -> p (c t)").bitcast(FP8X4),
                 scales=x_scales[m][:].rearrange("p c t -> p (c t)"),
-                in_=grouped[:],
+                in_=x_grouped[:],
             )
 
         def multiply(b):
@@ -161,7 +173,7 @@ def tile_groupqueryatention_pa_kernel(tc, x, angles, wq, wk, wv, out_0, out_1, o
             return banks
 
         pair_shape = [P, HEADS, HALF, 2]
-        banks = multiply(0)
+        banks = [multiply(b) for b in range(AHEAD)]
         for b in range(n_blocks):
             output, head, rotated = blocks[b][2], blocks[b][3], blocks[b][4]
             result = result_pool.tile([P, HEADS, TOKEN_TILES, HEAD], F32)
@@ -169,7 +181,7 @@ def tile_groupqueryatention_pa_kernel(tc, x, angles, wq, wk, wv, out_0, out_1, o
                 odd_part = odd_pool.tile([P, HEADS, TOKEN_TILES, HEAD], F32)
             for m in range(TOKEN_TILES):
                 if rotated:
-                    pairs = banks[m][:].rearrange("p (h i two) -> p h i two", h=HEADS, two=2)
+                    pairs = banks[b][m][:].rearrange("p (h i two) -> p h i two", h=HEADS, two=2)
                     for part, which in ((result, 0), (odd_part, 1)):
                         factors = trig[:, 1 - which : 3 - which, m, :].rearrange("p two i -> p i two")
                         nc.vector.tensor_tensor(
@@ -178,18 +190,32 @@ def tile_groupqueryatention_pa_kernel(tc, x, angles, wq, wk, wv, out_0, out_1, o
                             in1=factors.unsqueeze(1).to_broadcast(pair_shape),
                             op=ALU.mult,
                         )
+                    if m < GPSIMD_BANKS:
+                        nc.gpsimd.tensor_tensor(
+                            out=result[:, :, m, :],
+                            in0=result[:, :, m, :],
+                            in1=odd_part[:, :, m, :],
+                            op=ALU.add,
+                        )
                 else:
                     nc.scalar.copy(
                         out=result[:, :, m, :],
-                        in_=banks[m][:].rearrange("p (h f) -> p h f", h=HEADS),
+                        in_=banks[b][m][:].rearrange("p (h f) -> p h f", h=HEADS),
                     )
-                if b + 1 < n_blocks:
-                    prepare_chunk(b + 1, m)
+            if b + AHEAD < n_blocks:
+                for c in range(PASSES):
+                    regroup(b + AHEAD, c)
+                for c in range(PASSES):
+                    quantise(b + AHEAD, c)
             if rotated:
-                nc.vector.tensor_add(out=result[:], in0=result[:], in1=odd_part[:])
+                nc.vector.tensor_add(
+                    out=result[:, :, GPSIMD_BANKS:, :],
+                    in0=result[:, :, GPSIMD_BANKS:, :],
+                    in1=odd_part[:, :, GPSIMD_BANKS:, :],
+                )
             nc.sync.dma_start(
                 out=output[0, head : head + HEADS].rearrange("h (p m) f -> p h (m f)", m=TOKEN_TILES),
                 in_=result[:].rearrange("p h m f -> p h (m f)"),
             )
-            if b + 1 < n_blocks:
-                banks = multiply(b + 1)
+            if b + AHEAD < n_blocks:
+                banks.append(multiply(b + AHEAD))

@@ -25,6 +25,7 @@ TOKEN_TILES = TOKENS // P
 BLOCK = 512
 HEADS = BLOCK // HEAD
 RUN = 4
+JOINT = 2
 AHEAD = 2
 GPSIMD_BANKS = 2
 VECTOR_LAST_CHUNKS = 2
@@ -43,7 +44,7 @@ def tile_groupqueryatention_pa_kernel(tc, x, angles, wq, wk, wv, out_0, out_1, o
         consts = stack.enter_context(tc.tile_pool(name="consts", bufs=1))
         raw_pool = stack.enter_context(tc.tile_pool(name="raw", bufs=n_blocks * PASSES))
         x_grouped_pool = stack.enter_context(tc.tile_pool(name="x_grouped", bufs=2))
-        w_grouped_pool = stack.enter_context(tc.tile_pool(name="w_grouped", bufs=2 * PASSES))
+        w_grouped_pool = stack.enter_context(tc.tile_pool(name="w_grouped", bufs=2 * PASSES // JOINT))
         w_mx_pool = stack.enter_context(tc.tile_pool(name="w_mx", bufs=AHEAD))
         result_pool = stack.enter_context(tc.tile_pool(name="result", bufs=3))
         odd_pool = stack.enter_context(tc.tile_pool(name="odd", bufs=2))
@@ -101,34 +102,37 @@ def tile_groupqueryatention_pa_kernel(tc, x, angles, wq, wk, wv, out_0, out_1, o
         def regroup(b, c):
             on_vector = b == 0 or (c == PASSES - 1 and b <= VECTOR_LAST_CHUNKS)
             copy = nc.vector.tensor_copy if on_vector else nc.scalar.copy
-            w_grouped[b, c] = w_grouped_pool.tile(
-                [P, BLOCK, PACK], BF16, tag="w_grouped", name="w_grouped", align_bytes=64
-            )
+            if c % JOINT == 0:
+                w_grouped[b, c // JOINT] = w_grouped_pool.tile(
+                    [P, JOINT, BLOCK, PACK], BF16, tag="w_grouped", name="w_grouped", align_bytes=64
+                )
             copy(
-                out=w_grouped[b, c][:].rearrange("p (g i) j -> p g j i", i=RUN),
+                out=w_grouped[b, c // JOINT][:, c % JOINT].rearrange("p (g i) j -> p g j i", i=RUN),
                 in_=raw[b, c][:].rearrange("p j (g i) -> p g j i", i=RUN),
             )
 
-        def quantise(b, c):
-            if c == 0:
+        def quantise(b, first):
+            if first == 0:
                 w_codes[b] = w_mx_pool.tile(
                     [P, PASSES, BLOCK], U32, tag="w_codes", name="w_codes", align_bytes=64
                 )
                 w_scales[b] = w_mx_pool.tile(
                     [P, PASSES, BLOCK], U8, tag="w_scales", name="w_scales", align_bytes=64
                 )
+            chunks = slice(first, first + JOINT)
             nc.vector.quantize_mx(
-                out=w_codes[b][:, c, :].bitcast(FP8X4),
-                scales=w_scales[b][:, c, :],
-                in_=w_grouped[b, c][:].rearrange("p n j -> p (n j)"),
+                out=w_codes[b][:, chunks, :].rearrange("p c n -> p (c n)").bitcast(FP8X4),
+                scales=w_scales[b][:, chunks, :].rearrange("p c n -> p (c n)"),
+                in_=w_grouped[b, first // JOINT][:].rearrange("p c n j -> p (c n j)"),
             )
 
-        for c in range(PASSES):
-            for b in range(AHEAD):
-                regroup(b, c)
-            quantise(0, c)
-        for c in range(PASSES):
-            quantise(1, c)
+        for first in range(0, PASSES, JOINT):
+            for c in range(first, first + JOINT):
+                for b in range(AHEAD):
+                    regroup(b, c)
+            quantise(0, first)
+        for first in range(0, PASSES, JOINT):
+            quantise(1, first)
 
         x_codes = []
         x_scales = []
@@ -177,6 +181,7 @@ def tile_groupqueryatention_pa_kernel(tc, x, angles, wq, wk, wv, out_0, out_1, o
         for b in range(n_blocks):
             output, head, rotated = blocks[b][2], blocks[b][3], blocks[b][4]
             result = result_pool.tile([P, HEADS, TOKEN_TILES, HEAD], F32)
+            stored = output[0, head : head + HEADS].rearrange("h (p m) f -> p h m f", m=TOKEN_TILES)
             if rotated:
                 odd_part = odd_pool.tile([P, HEADS, TOKEN_TILES, HEAD], F32)
             for m in range(TOKEN_TILES):
@@ -202,20 +207,18 @@ def tile_groupqueryatention_pa_kernel(tc, x, angles, wq, wk, wv, out_0, out_1, o
                         out=result[:, :, m, :],
                         in_=banks[b][m][:].rearrange("p (h f) -> p h f", h=HEADS),
                     )
+            nc.sync.dma_start(out=stored[:, :, :GPSIMD_BANKS, :], in_=result[:, :, :GPSIMD_BANKS, :])
             if b + AHEAD < n_blocks:
                 for c in range(PASSES):
                     regroup(b + AHEAD, c)
-                for c in range(PASSES):
-                    quantise(b + AHEAD, c)
+                for first in range(0, PASSES, JOINT):
+                    quantise(b + AHEAD, first)
             if rotated:
                 nc.vector.tensor_add(
                     out=result[:, :, GPSIMD_BANKS:, :],
                     in0=result[:, :, GPSIMD_BANKS:, :],
                     in1=odd_part[:, :, GPSIMD_BANKS:, :],
                 )
-            nc.sync.dma_start(
-                out=output[0, head : head + HEADS].rearrange("h (p m) f -> p h (m f)", m=TOKEN_TILES),
-                in_=result[:].rearrange("p h m f -> p h (m f)"),
-            )
+            nc.sync.dma_start(out=stored[:, :, GPSIMD_BANKS:, :], in_=result[:, :, GPSIMD_BANKS:, :])
             if b + AHEAD < n_blocks:
                 banks.append(multiply(b + AHEAD))

@@ -25,7 +25,6 @@ TOKEN_TILES = TOKENS // P
 BLOCK = 512
 HEADS = BLOCK // HEAD
 RUN = 4
-JOINT = 2
 AHEAD = 2
 GPSIMD_BANKS = 2
 VECTOR_LAST_CHUNKS = 2
@@ -44,7 +43,7 @@ def tile_groupqueryatention_pa_kernel(tc, x, angles, wq, wk, wv, out_0, out_1, o
         consts = stack.enter_context(tc.tile_pool(name="consts", bufs=1))
         raw_pool = stack.enter_context(tc.tile_pool(name="raw", bufs=n_blocks * PASSES))
         x_grouped_pool = stack.enter_context(tc.tile_pool(name="x_grouped", bufs=2))
-        w_grouped_pool = stack.enter_context(tc.tile_pool(name="w_grouped", bufs=2 * PASSES // JOINT))
+        w_grouped_pool = stack.enter_context(tc.tile_pool(name="w_grouped", bufs=2 * PASSES))
         w_mx_pool = stack.enter_context(tc.tile_pool(name="w_mx", bufs=AHEAD))
         result_pool = stack.enter_context(tc.tile_pool(name="result", bufs=3))
         odd_pool = stack.enter_context(tc.tile_pool(name="odd", bufs=2))
@@ -102,37 +101,34 @@ def tile_groupqueryatention_pa_kernel(tc, x, angles, wq, wk, wv, out_0, out_1, o
         def regroup(b, c):
             on_vector = b == 0 or (c == PASSES - 1 and b <= VECTOR_LAST_CHUNKS)
             copy = nc.vector.tensor_copy if on_vector else nc.scalar.copy
-            if c % JOINT == 0:
-                w_grouped[b, c // JOINT] = w_grouped_pool.tile(
-                    [P, JOINT, BLOCK, PACK], BF16, tag="w_grouped", name="w_grouped", align_bytes=64
-                )
+            w_grouped[b, c] = w_grouped_pool.tile(
+                [P, BLOCK, PACK], BF16, tag="w_grouped", name="w_grouped", align_bytes=64
+            )
             copy(
-                out=w_grouped[b, c // JOINT][:, c % JOINT].rearrange("p (g i) j -> p g j i", i=RUN),
+                out=w_grouped[b, c][:].rearrange("p (g i) j -> p g j i", i=RUN),
                 in_=raw[b, c][:].rearrange("p j (g i) -> p g j i", i=RUN),
             )
 
-        def quantise(b, first):
-            if first == 0:
+        def quantise(b, c):
+            if c == 0:
                 w_codes[b] = w_mx_pool.tile(
                     [P, PASSES, BLOCK], U32, tag="w_codes", name="w_codes", align_bytes=64
                 )
                 w_scales[b] = w_mx_pool.tile(
                     [P, PASSES, BLOCK], U8, tag="w_scales", name="w_scales", align_bytes=64
                 )
-            chunks = slice(first, first + JOINT)
             nc.vector.quantize_mx(
-                out=w_codes[b][:, chunks, :].rearrange("p c n -> p (c n)").bitcast(FP8X4),
-                scales=w_scales[b][:, chunks, :].rearrange("p c n -> p (c n)"),
-                in_=w_grouped[b, first // JOINT][:].rearrange("p c n j -> p (c n j)"),
+                out=w_codes[b][:, c, :].bitcast(FP8X4),
+                scales=w_scales[b][:, c, :],
+                in_=w_grouped[b, c][:].rearrange("p n j -> p (n j)"),
             )
 
-        for first in range(0, PASSES, JOINT):
-            for c in range(first, first + JOINT):
-                for b in range(AHEAD):
-                    regroup(b, c)
-            quantise(0, first)
-        for first in range(0, PASSES, JOINT):
-            quantise(1, first)
+        for c in range(PASSES):
+            for b in range(AHEAD):
+                regroup(b, c)
+            quantise(0, c)
+        for c in range(PASSES):
+            quantise(1, c)
 
         x_codes = []
         x_scales = []
@@ -211,8 +207,8 @@ def tile_groupqueryatention_pa_kernel(tc, x, angles, wq, wk, wv, out_0, out_1, o
             if b + AHEAD < n_blocks:
                 for c in range(PASSES):
                     regroup(b + AHEAD, c)
-                for first in range(0, PASSES, JOINT):
-                    quantise(b + AHEAD, first)
+                for c in range(PASSES):
+                    quantise(b + AHEAD, c)
             if rotated:
                 nc.vector.tensor_add(
                     out=result[:, :, GPSIMD_BANKS:, :],

@@ -28,6 +28,9 @@ RUN = 4
 AHEAD = 2
 GPSIMD_BANKS = 2
 VECTOR_LAST_CHUNKS = 2
+RAW_TILES = 20
+HEAD_WARM_UPS = 3
+TAIL_WARM_UPS = 6
 
 FLOPS = 2 * TOKENS * K * (Q_COLUMNS + 2 * KV_COLUMNS)
 
@@ -41,8 +44,8 @@ def tile_groupqueryatention_pa_kernel(tc, x, angles, wq, wk, wv, out_0, out_1, o
 
     with ExitStack() as stack:
         consts = stack.enter_context(tc.tile_pool(name="consts", bufs=1))
-        raw_pool = stack.enter_context(tc.tile_pool(name="raw", bufs=n_blocks * PASSES))
-        x_grouped_pool = stack.enter_context(tc.tile_pool(name="x_grouped", bufs=2))
+        raw_pool = stack.enter_context(tc.tile_pool(name="raw", bufs=RAW_TILES))
+        x_grouped_pool = stack.enter_context(tc.tile_pool(name="x_grouped", bufs=TOKEN_TILES))
         w_grouped_pool = stack.enter_context(tc.tile_pool(name="w_grouped", bufs=2 * PASSES))
         w_mx_pool = stack.enter_context(tc.tile_pool(name="w_mx", bufs=AHEAD))
         result_pool = stack.enter_context(tc.tile_pool(name="result", bufs=3))
@@ -75,6 +78,8 @@ def tile_groupqueryatention_pa_kernel(tc, x, angles, wq, wk, wv, out_0, out_1, o
 
         identity = consts.tile([P, P], F32)
         make_identity(nc, identity[:])
+        identity_bf16 = consts.tile([P, P], BF16)
+        make_identity(nc, identity_bf16[:])
 
         trig = consts.tile([P, 3, TOKEN_TILES, HALF], F32)
         sin_half = consts.tile([P, TOKEN_TILES, HALF], F32)
@@ -155,10 +160,19 @@ def tile_groupqueryatention_pa_kernel(tc, x, angles, wq, wk, wv, out_0, out_1, o
                 in_=x_grouped[:],
             )
 
-        def multiply(b):
+        def multiply(b, warm_on=None, warm_ups=0):
             banks = []
             for m in range(TOKEN_TILES):
                 acc = psum.tile([P, BLOCK], F32, tag="bank")
+                if m == 0 and warm_on is not None:
+                    for i in range(warm_ups):
+                        nc.tensor.matmul(
+                            out=acc[:],
+                            lhsT=identity_bf16[:],
+                            rhs=warm_on[:].rearrange("p n j -> p (n j)")[:, :BLOCK],
+                            start=True,
+                            stop=True,
+                        )
                 for c in range(PASSES):
                     nc.tensor.matmul_mx(
                         out=acc[:],
@@ -173,7 +187,7 @@ def tile_groupqueryatention_pa_kernel(tc, x, angles, wq, wk, wv, out_0, out_1, o
             return banks
 
         pair_shape = [P, HEADS, HALF, 2]
-        banks = [multiply(b) for b in range(AHEAD)]
+        banks = [multiply(0, w_grouped[1, PASSES - 1], HEAD_WARM_UPS), multiply(1)]
         for b in range(n_blocks):
             output, head, rotated = blocks[b][2], blocks[b][3], blocks[b][4]
             result = result_pool.tile([P, HEADS, TOKEN_TILES, HEAD], F32)
@@ -217,4 +231,5 @@ def tile_groupqueryatention_pa_kernel(tc, x, angles, wq, wk, wv, out_0, out_1, o
                 )
             nc.sync.dma_start(out=stored[:, :, GPSIMD_BANKS:, :], in_=result[:, :, GPSIMD_BANKS:, :])
             if b + AHEAD < n_blocks:
-                banks.append(multiply(b + AHEAD))
+                last = b + AHEAD == n_blocks - 1
+                banks.append(multiply(b + AHEAD, w_grouped[b + AHEAD, PASSES - 2] if last else None, TAIL_WARM_UPS))

@@ -223,13 +223,16 @@ def tile_groupqueryatention_pa_kernel(tc, x, angles, wq, wk, wv, out_0, out_1, o
                     regroup(b + AHEAD, c)
                 for c in range(PASSES):
                     quantise(b + AHEAD, c)
-            if rotated:
-                nc.vector.tensor_add(
-                    out=result[:, :, GPSIMD_BANKS:, :],
-                    in0=result[:, :, GPSIMD_BANKS:, :],
-                    in1=odd_part[:, :, GPSIMD_BANKS:, :],
-                )
-            nc.sync.dma_start(out=stored[:, :, GPSIMD_BANKS:, :], in_=result[:, :, GPSIMD_BANKS:, :])
+            step = 1 if b == n_blocks - 1 else TOKEN_TILES - GPSIMD_BANKS
+            for first in range(GPSIMD_BANKS, TOKEN_TILES, step):
+                tiles = slice(first, first + step)
+                if rotated:
+                    nc.vector.tensor_add(
+                        out=result[:, :, tiles, :],
+                        in0=result[:, :, tiles, :],
+                        in1=odd_part[:, :, tiles, :],
+                    )
+                nc.sync.dma_start(out=stored[:, :, tiles, :], in_=result[:, :, tiles, :])
             if b + AHEAD < n_blocks:
                 last = b + AHEAD == n_blocks - 1
                 banks.append(multiply(b + AHEAD, w_grouped[b + AHEAD, PASSES - 2] if last else None, TAIL_WARM_UPS))

from contextlib import ExitStack

import concourse.mybir as mybir
from concourse.masks import make_identity

F32 = mybir.dt.float32
BF16 = mybir.dt.bfloat16
U32 = mybir.dt.uint32
U8 = mybir.dt.uint8
FP8X4 = mybir.dt.float8_e4m3fn_x4
ACT = mybir.ActivationFunctionType
ALU = mybir.AluOpType

P = 128
PACK = 4
K_PASS = P * PACK
TOKENS = 512
K = 2048
HEAD = 128
HALF = HEAD // 2
Q_COLUMNS = 2048
KV_COLUMNS = 512
PASSES = K // K_PASS
TOKEN_TILES = TOKENS // P
BLOCK = 512
HEADS = BLOCK // HEAD
RUN = 4
AHEAD = 2
GPSIMD_BANKS = 2
VECTOR_LAST_CHUNKS = 2
RAW_TILES = 20
HEAD_WARM_UPS = 3
TAIL_WARM_UPS = 6

FLOPS = 2 * TOKENS * K * (Q_COLUMNS + 2 * KV_COLUMNS)


def tile_groupqueryatention_pa_kernel(tc, x, angles, wq, wk, wv, out_0, out_1, out_2):
    nc = tc.nc

    q_blocks = [(wq, g * BLOCK, out_0, g * HEADS, True) for g in range(Q_COLUMNS // BLOCK)]
    blocks = [(wk, 0, out_1, 0, True)] + q_blocks[:-1] + [(wv, 0, out_2, 0, False)] + q_blocks[-1:]
    n_blocks = len(blocks)

    with ExitStack() as stack:
        consts = stack.enter_context(tc.tile_pool(name="consts", bufs=1))
        raw_pool = stack.enter_context(tc.tile_pool(name="raw", bufs=RAW_TILES))
        x_grouped_pool = stack.enter_context(tc.tile_pool(name="x_grouped", bufs=TOKEN_TILES))
        w_grouped_pool = stack.enter_context(tc.tile_pool(name="w_grouped", bufs=2 * PASSES))
        w_mx_pool = stack.enter_context(tc.tile_pool(name="w_mx", bufs=AHEAD))
        result_pool = stack.enter_context(tc.tile_pool(name="result", bufs=3))
        odd_pool = stack.enter_context(tc.tile_pool(name="odd", bufs=2))
        psum = stack.enter_context(tc.psum_pool(name="psum", bufs=AHEAD * TOKEN_TILES))
        stack.enter_context(tc.manual_schedule())

        angle = consts.tile([P, TOKEN_TILES, HALF], BF16)
        nc.sync.dma_start(out=angle[:], in_=angles.rearrange("(p m) i -> p m i", m=TOKEN_TILES))

        raw = {}

        def load_chunk(b, c):
            weight, column = blocks[b][0], blocks[b][1]
            rows = weight[c * K_PASS : (c + 1) * K_PASS, column : column + BLOCK]
            raw[b, c] = raw_pool.tile([P, PACK, BLOCK], BF16, tag="raw", name="raw")
            nc.sync.dma_start(out=raw[b, c][:], in_=rows.rearrange("(p j) n -> p j n", j=PACK))

        for c in range(PASSES):
            for b in range(AHEAD):
                load_chunk(b, c)
        x_tokens = x[0].rearrange("(p m) k -> p m k", m=TOKEN_TILES)
        x_sb = []
        for m in range(TOKEN_TILES):
            x_sb.append(consts.tile([P, K], BF16, name="x_sb%d" % m))
            nc.sync.dma_start(out=x_sb[m][:], in_=x_tokens[:, m, :])
        for b in range(AHEAD, n_blocks):
            for c in range(PASSES):
                load_chunk(b, c)

        identity = consts.tile([P, P], F32)
        make_identity(nc, identity[:])
        identity_bf16 = consts.tile([P, P], BF16)
        make_identity(nc, identity_bf16[:])

        trig = consts.tile([P, 3, TOKEN_TILES, HALF], F32)
        sin_half = consts.tile([P, TOKEN_TILES, HALF], F32)
        sin_half_squared = consts.tile([P, TOKEN_TILES, HALF], F32)
        nc.scalar.activation(out=trig[:, 0], in_=angle[:], func=ACT.Sin, scale=-1.0)
        nc.scalar.activation(out=trig[:, 2], in_=angle[:], func=ACT.Sin)
        nc.scalar.activation(out=sin_half[:], in_=angle[:], func=ACT.Sin, scale=0.5)
        nc.gpsimd.tensor_tensor(
            out=sin_half_squared[:], in0=sin_half[:], in1=sin_half[:], op=ALU.mult
        )
        nc.gpsimd.tensor_scalar(
            out=trig[:, 1],
            in0=sin_half_squared[:],
            scalar1=-2.0,
            scalar2=1.0,
            op0=ALU.mult,
            op1=ALU.add,
        )

        w_grouped = {}
        w_codes = {}
        w_scales = {}

        def regroup(b, c):
            on_vector = b == 0 or (c == PASSES - 1 and b <= VECTOR_LAST_CHUNKS)
            copy = nc.vector.tensor_copy if on_vector else nc.scalar.copy
            w_grouped[b, c] = w_grouped_pool.tile(
                [P, BLOCK, PACK], BF16, tag="w_grouped", name="w_grouped", align_bytes=64
            )
            copy(
                out=w_grouped[b, c][:].rearrange("p (g i) j -> p g j i", i=RUN),
                in_=raw[b, c][:].rearrange("p j (g i) -> p g j i", i=RUN),
            )

        def quantise(b, c):
            if c == 0:
                w_codes[b] = w_mx_pool.tile(
                    [P, PASSES, BLOCK], U32, tag="w_codes", name="w_codes", align_bytes=64
                )
                w_scales[b] = w_mx_pool.tile(
                    [P, PASSES, BLOCK], U8, tag="w_scales", name="w_scales", align_bytes=64
                )
            nc.vector.quantize_mx(
                out=w_codes[b][:, c, :].bitcast(FP8X4),
                scales=w_scales[b][:, c, :],
                in_=w_grouped[b, c][:].rearrange("p n j -> p (n j)"),
            )

        for c in range(PASSES):
            for b in range(AHEAD):
                regroup(b, c)
            quantise(0, c)
        for c in range(PASSES):
            quantise(1, c)

        x_codes = []
        x_scales = []
        for m in range(TOKEN_TILES):
            x_words = x_sb[m][:].bitcast(F32).rearrange("p (c q u) -> p c u q", c=PASSES, u=2)
            x_grouped = x_grouped_pool.tile([P, PASSES * P * PACK], BF16, align_bytes=64)
            grouped_words = x_grouped[:].bitcast(F32).rearrange(
                "p (c t u) -> p c t u", c=PASSES, u=2
            )
            for first in range(0, PASSES, 2):
                bank = psum.tile([P, 2, 2, P], F32, tag="bank")
                for c in range(2):
                    for u in range(2):
                        nc.tensor.transpose(bank[:, c, u, :], x_words[:, first + c, u, :], identity[:])
                nc.scalar.copy(
                    out=grouped_words[:, first : first + 2],
                    in_=bank[:].rearrange("p c u t -> p c t u"),
                )
            x_codes.append(consts.tile([P, PASSES, P], U32, name="x_codes%d" % m, align_bytes=64))
            x_scales.append(consts.tile([P, PASSES, P], U8, name="x_scales%d" % m, align_bytes=64))
            nc.vector.quantize_mx(
                out=x_codes[m][:].rearrange("p c t -> p (c t)").bitcast(FP8X4),
                scales=x_scales[m][:].rearrange("p c t -> p (c t)"),
                in_=x_grouped[:],
            )

        def multiply(b, warm_on=None, warm_ups=0):
            banks = []
            for m in range(TOKEN_TILES):
                acc = psum.tile([P, BLOCK], F32, tag="bank")
                if m == 0 and warm_on is not None:
                    for i in range(warm_ups):
                        nc.tensor.matmul(
                            out=acc[:],
                            lhsT=identity_bf16[:],
                            rhs=warm_on[:].rearrange("p n j -> p (n j)")[:, :BLOCK],
                            start=True,
                            stop=True,
                        )
                for c in range(PASSES):
                    nc.tensor.matmul_mx(
                        out=acc[:],
                        lhsT=x_codes[m][:, c, :].bitcast(FP8X4),
                        lhsT_scale=x_scales[m][:, c, :],
                        rhs=w_codes[b][:, c, :].bitcast(FP8X4),
                        rhs_scale=w_scales[b][:, c, :],
                        start=(c == 0),
                        stop=(c == PASSES - 1),
                    )
                banks.append(acc)
            return banks

        pair_shape = [P, HEADS, HALF, 2]
        banks = [multiply(0, w_grouped[1, PASSES - 1], HEAD_WARM_UPS), multiply(1)]
        for b in range(n_blocks):
            output, head, rotated = blocks[b][2], blocks[b][3], blocks[b][4]
            result = result_pool.tile([P, HEADS, TOKEN_TILES, HEAD], F32)
            stored = output[0, head : head + HEADS].rearrange("h (p m) f -> p h m f", m=TOKEN_TILES)
            if rotated:
                odd_part = odd_pool.tile([P, HEADS, TOKEN_TILES, HEAD], F32)
            for m in range(TOKEN_TILES):
                if rotated:
                    pairs = banks[b][m][:].rearrange("p (h i two) -> p h i two", h=HEADS, two=2)
                    for part, which in ((result, 0), (odd_part, 1)):
                        factors = trig[:, 1 - which : 3 - which, m, :].rearrange("p two i -> p i two")
                        nc.vector.tensor_tensor(
                            out=part[:, :, m, :].rearrange("p h (i two) -> p h i two", two=2),
                            in0=pairs[:, :, :, which : which + 1].to_broadcast(pair_shape),
                            in1=factors.unsqueeze(1).to_broadcast(pair_shape),
                            op=ALU.mult,
                        )
                    if m < GPSIMD_BANKS:
                        nc.gpsimd.tensor_tensor(
                            out=result[:, :, m, :],
                            in0=result[:, :, m, :],
                            in1=odd_part[:, :, m, :],
                            op=ALU.add,
                        )
                else:
                    nc.scalar.copy(
                        out=result[:, :, m, :],
                        in_=banks[b][m][:].rearrange("p (h f) -> p h f", h=HEADS),
                    )
            nc.sync.dma_start(out=stored[:, :, :GPSIMD_BANKS, :], in_=result[:, :, :GPSIMD_BANKS, :])
            if b + AHEAD < n_blocks:
                for c in range(PASSES):
                    regroup(b + AHEAD, c)
                for c in range(PASSES):
                    quantise(b + AHEAD, c)
            step = 1 if b == n_blocks - 1 else TOKEN_TILES - GPSIMD_BANKS
            for first in range(GPSIMD_BANKS, TOKEN_TILES, step):
                tiles = slice(first, first + step)
                if rotated:
                    nc.vector.tensor_add(
                        out=result[:, :, tiles, :],
                        in0=result[:, :, tiles, :],
                        in1=odd_part[:, :, tiles, :],
                    )
                nc.sync.dma_start(out=stored[:, :, tiles, :], in_=result[:, :, tiles, :])
            if b + AHEAD < n_blocks:
                last = b + AHEAD == n_blocks - 1
                banks.append(multiply(b + AHEAD, w_grouped[b + AHEAD, PASSES - 2] if last else None, TAIL_WARM_UPS))
